import numpy as np
import ml_dtypes


def mxq(x, axis, fmt="e4m3"):
    dtype, down = {"e4m3": (ml_dtypes.float8_e4m3fn, 7), "e5m2": (ml_dtypes.float8_e5m2, 14)}[fmt]
    v = np.moveaxis(np.asarray(x, np.float32).astype(ml_dtypes.bfloat16).astype(np.float64), axis, -1)
    blocks = v.reshape(v.shape[:-1] + (-1, 32))
    amax = np.abs(blocks).max(-1, keepdims=True)
    byte = np.maximum(np.where(amax > 0, np.frexp(amax)[1] - 1 + 127, 0) - down, 1)
    scale = np.exp2(byte - 127.0)
    codes = (blocks / scale).astype(np.float32).astype(dtype).astype(np.float64)
    return np.moveaxis((codes * scale).reshape(v.shape), -1, axis)


WIDE = False


def mx_kscale(k):
    if not WIDE:
        return np.ones(k)
    levels = np.array([20, -20, 10, -10, 0])
    a = np.random.permutation(np.resize(levels, k // 512 * 4)).reshape(k // 512, 4)
    idx = np.arange(k)
    return np.exp2(a[idx // 512, idx % 128 // 32])


BF16 = ml_dtypes.bfloat16


def bf(x):
    return np.asarray(x, np.float32).astype(BF16)


def f64(x):
    return np.asarray(x).astype(np.float64)


N, C, F, H, W, KH, KW = 128, 64, 512, 4, 4, 3, 3
P = H * W


def setup_inputs():
    u = mx_kscale(F)
    x = np.random.standard_normal((N, C, H, W)) * 2.0
    k = np.random.standard_normal((F, C, H, W)) * 2.0 / np.sqrt(C) / u[:, None, None, None]
    g = (np.random.standard_normal((N, F, H, W)) * np.exp2(np.random.randint(-12, 1, (N, 1, H, W)))
         * 4.0 * u[None, :, None, None])
    return {"x_dct": bf(x), "k_dct": bf(k), "grad_out": bf(g)}


def reference(x_dct, k_dct, grad_out):
    gq = mxq(f64(grad_out), 1, "e5m2").reshape(N, F, P).transpose(2, 0, 1)
    kq = mxq(f64(k_dct), 0, "e4m3").reshape(F, C, P).transpose(2, 0, 1)
    r = gq @ kq
    return r.transpose(1, 2, 0).reshape(N, C, H, W)

@@ -1,0 +1,127 @@
+from contextlib import ExitStack
+
+import concourse.mybir as mybir
+from concourse.masks import make_identity
+
+BF16 = mybir.dt.bfloat16
+F32 = mybir.dt.float32
+I32 = mybir.dt.int32
+U32 = mybir.dt.uint32
+U8 = mybir.dt.uint8
+E5M2_X4 = mybir.dt.float8_e5m2_x4
+E4M3_X4 = mybir.dt.float8_e4m3fn_x4
+
+IMAGES = 128
+CHANNELS = 64
+FILTERS = 512
+FREQS = 16
+
+P = 128
+PACK = 4
+CHUNK_IMAGES = P // PACK
+CHUNKS = IMAGES // CHUNK_IMAGES
+GROUP = 4
+GROUPS = FREQS // GROUP
+PAIRS = GROUP // 2
+WORDS_PER_FILTER = FREQS // 2
+N_MOVING = 512
+GAP = (GROUP - 1) * CHANNELS
+PITCH = CHANNELS + GAP
+STRIP = (GROUP - 1) * GAP + N_MOVING
+
+FLOPS = 2 * IMAGES * CHANNELS * FILTERS * FREQS
+BYTES = 2 * IMAGES * FILTERS * FREQS + 2 * FILTERS * CHANNELS * FREQS + 4 * IMAGES * CHANNELS * FREQS
+
+
+def tile_convdct_pa_s_kernel(tc, x_dct, k_dct, grad_out, out):
+    nc = tc.nc
+    with ExitStack() as ctx:
+        keep = ctx.enter_context(tc.tile_pool(name="keep", bufs=1))
+        turned_pool = ctx.enter_context(tc.psum_pool(name="turned_pool", bufs=4))
+        acc_pool = ctx.enter_context(tc.psum_pool(name="acc_pool", bufs=4))
+
+        g_rows = grad_out.rearrange("n (t q) h w -> (n t) (q h w)", t=PACK)
+        g_raw = []
+        for c in range(CHUNKS):
+            raw = keep.tile([P, P * FREQS], BF16, name="g_raw%d" % c)
+            nc.sync.dma_start(out=raw[:], in_=g_rows[c * P : (c + 1) * P, :])
+            g_raw.append(raw)
+        k_raw = keep.tile([P, PACK, CHANNELS * FREQS], BF16, name="k_raw")
+        nc.sync.dma_start(out=k_raw[:], in_=k_dct.rearrange("(t q) c h w -> q t (c h w)", q=P))
+
+        ident = keep.tile([P, P], F32, name="ident")
+        make_identity(nc, ident[:])
+
+        k_codes = []
+        k_scales = []
+        for g in range(GROUPS):
+            codes = keep.tile([P, STRIP], U32, name="k_codes%d" % g, align_bytes=64)
+            scales = keep.tile([P, STRIP], U8, name="k_scales%d" % g, align_bytes=64)
+            nc.vector.memset(codes[:].bitcast(I32), 0)
+            nc.vector.memset(scales[:].bitcast(I32), 0)
+            k_codes.append(codes)
+            k_scales.append(scales)
+
+        g_grouped = []
+        for g in range(GROUPS):
+            grouped = keep.tile([P, GROUP, IMAGES * PACK], BF16, name="g_grouped%d" % g, align_bytes=64)
+            g_grouped.append(grouped)
+        for c in range(CHUNKS):
+            words = g_raw[c][:].bitcast(F32).rearrange("r (q w) -> r w q", w=WORDS_PER_FILTER)
+            for g in range(GROUPS):
+                turned = turned_pool.tile([P, PAIRS * P], F32, name="turned")
+                for j in range(PAIRS):
+                    nc.tensor.transpose(turned[:, j * P : (j + 1) * P], words[:, g * PAIRS + j, :], ident[:])
+                src = turned[:].bitcast(BF16).rearrange("q (j m e) -> q j e m", j=PAIRS, e=2)
+                dst = g_grouped[g][:, :, c * P : (c + 1) * P].rearrange("q (j e) m -> q j e m", e=2)
+                if g % 2 == 0:
+                    nc.vector.tensor_copy(out=dst, in_=src)
+                else:
+                    nc.scalar.copy(out=dst, in_=src)
+
+        g_codes = []
+        g_scales = []
+        for g in range(GROUPS):
+            codes = keep.tile([P, GROUP * IMAGES], U32, name="g_codes%d" % g, align_bytes=64)
+            scales = keep.tile([P, GROUP * IMAGES], U8, name="g_scales%d" % g, align_bytes=64)
+            nc.vector.quantize_mx(
+                out=codes[:].bitcast(E5M2_X4),
+                scales=scales[:],
+                in_=g_grouped[g][:].rearrange("q p m -> q (p m)"),
+            )
+            g_codes.append(codes)
+            g_scales.append(scales)
+
+        k_view = k_raw[:].rearrange("q t (c p) -> q p c t", p=FREQS)
+        out_sb = keep.tile([P, CHANNELS, FREQS], F32, name="out_sb")
+        half = GROUP // 2
+        for g in range(GROUPS):
+            first = g * GROUP
+            k_grouped = keep.tile([P, GROUP, CHANNELS, PACK], BF16, name="k_grouped%d" % g, align_bytes=64)
+            nc.vector.tensor_copy(out=k_grouped[:, :half], in_=k_view[:, first : first + half])
+            nc.scalar.copy(out=k_grouped[:, half:], in_=k_view[:, first + half : first + GROUP])
+            for b in range(GROUP):
+                nc.vector.quantize_mx(
+                    out=k_codes[g][:, b * PITCH : b * PITCH + CHANNELS].bitcast(E4M3_X4),
+                    scales=k_scales[g][:, b * PITCH : b * PITCH + CHANNELS],
+                    in_=k_grouped[:, b].rearrange("q c t -> q (c t)"),
+                )
+            acc = acc_pool.tile([P, N_MOVING], F32, name="acc")
+            for b in range(GROUP):
+                window = slice(b * GAP, b * GAP + N_MOVING)
+                nc.tensor.matmul_mx(
+                    out=acc[:],
+                    lhsT=g_codes[g][:, b * IMAGES : (b + 1) * IMAGES].bitcast(E5M2_X4),
+                    lhsT_scale=g_scales[g][:, b * IMAGES : (b + 1) * IMAGES],
+                    rhs=k_codes[g][:, window].bitcast(E4M3_X4),
+                    rhs_scale=k_scales[g][:, window],
+                    start=(b == 0),
+                    stop=(b == GROUP - 1),
+                )
+            products = acc[:, : GROUP * CHANNELS].rearrange("n (b c) -> n c b", b=GROUP)
+            if g < GROUPS // 2:
+                nc.vector.tensor_copy(out=out_sb[:, :, first : first + GROUP], in_=products)
+            else:
+                nc.scalar.copy(out=out_sb[:, :, first : first + GROUP], in_=products)
+
+        nc.sync.dma_start(out=out.rearrange("n c h w -> n (c h w)"), in_=out_sb[:].rearrange("n c p -> n (c p)"))

@@ -20,14 +20,17 @@ P = 128
 PACK = 4
 CHUNK_IMAGES = P // PACK
 CHUNKS = IMAGES // CHUNK_IMAGES
+WORDS_PER_FILTER = FREQS // 2
+BANK_PAIRS = 4
+BANK_FREQS = 2 * BANK_PAIRS
+BANKS = FREQS // BANK_FREQS
 GROUP = 4
 GROUPS = FREQS // GROUP
-PAIRS = GROUP // 2
-WORDS_PER_FILTER = FREQS // 2
 N_MOVING = 512
 GAP = (GROUP - 1) * CHANNELS
 PITCH = CHANNELS + GAP
 STRIP = (GROUP - 1) * GAP + N_MOVING
+K_ON_VECTOR = 1
 
 FLOPS = 2 * IMAGES * CHANNELS * FILTERS * FREQS
 BYTES = 2 * IMAGES * FILTERS * FREQS + 2 * FILTERS * CHANNELS * FREQS + 4 * IMAGES * CHANNELS * FREQS
@@ -36,9 +39,10 @@ BYTES = 2 * IMAGES * FILTERS * FREQS + 2 * FILTERS * CHANNELS * FREQS + 4 * IMAG
 def tile_convdct_pa_s_kernel(tc, x_dct, k_dct, grad_out, out):
     nc = tc.nc
     with ExitStack() as ctx:
+        ctx.enter_context(tc.manual_schedule())
         keep = ctx.enter_context(tc.tile_pool(name="keep", bufs=1))
         turned_pool = ctx.enter_context(tc.psum_pool(name="turned_pool", bufs=4))
-        acc_pool = ctx.enter_context(tc.psum_pool(name="acc_pool", bufs=4))
+        acc_pool = ctx.enter_context(tc.psum_pool(name="acc_pool", bufs=GROUPS))
 
         g_rows = grad_out.rearrange("n (t q) h w -> (n t) (q h w)", t=PACK)
         g_raw = []
@@ -63,49 +67,55 @@ def tile_convdct_pa_s_kernel(tc, x_dct, k_dct, grad_out, out):
             k_scales.append(scales)
 
         g_grouped = []
-        for g in range(GROUPS):
-            grouped = keep.tile([P, GROUP, IMAGES * PACK], BF16, name="g_grouped%d" % g, align_bytes=64)
+        for h in range(BANKS):
+            grouped = keep.tile([P, BANK_FREQS, IMAGES * PACK], BF16, name="g_grouped%d" % h, align_bytes=64)
             g_grouped.append(grouped)
         for c in range(CHUNKS):
             words = g_raw[c][:].bitcast(F32).rearrange("r (q w) -> r w q", w=WORDS_PER_FILTER)
-            for g in range(GROUPS):
-                turned = turned_pool.tile([P, PAIRS * P], F32, name="turned")
-                for j in range(PAIRS):
-                    nc.tensor.transpose(turned[:, j * P : (j + 1) * P], words[:, g * PAIRS + j, :], ident[:])
-                src = turned[:].bitcast(BF16).rearrange("q (j m e) -> q j e m", j=PAIRS, e=2)
-                dst = g_grouped[g][:, :, c * P : (c + 1) * P].rearrange("q (j e) m -> q j e m", e=2)
-                if g % 2 == 0:
+            for h in range(BANKS):
+                turned = turned_pool.tile([P, BANK_PAIRS * P], F32, name="turned")
+                for j in range(BANK_PAIRS):
+                    nc.tensor.transpose(turned[:, j * P : (j + 1) * P], words[:, h * BANK_PAIRS + j, :], ident[:])
+                src = turned[:].bitcast(BF16).rearrange("q (j m e) -> q j e m", j=BANK_PAIRS, e=2)
+                dst = g_grouped[h][:, :, c * P : (c + 1) * P].rearrange("q (j e) m -> q j e m", e=2)
+                if h % 2 == 0:
                     nc.vector.tensor_copy(out=dst, in_=src)
                 else:
                     nc.scalar.copy(out=dst, in_=src)
 
         g_codes = []
         g_scales = []
+        k_grouped = []
         for g in range(GROUPS):
-            codes = keep.tile([P, GROUP * IMAGES], U32, name="g_codes%d" % g, align_bytes=64)
-            scales = keep.tile([P, GROUP * IMAGES], U8, name="g_scales%d" % g, align_bytes=64)
-            nc.vector.quantize_mx(
-                out=codes[:].bitcast(E5M2_X4),
-                scales=scales[:],
-                in_=g_grouped[g][:].rearrange("q p m -> q (p m)"),
-            )
-            g_codes.append(codes)
-            g_scales.append(scales)
-
+            g_codes.append(keep.tile([P, GROUP * IMAGES], U32, name="g_codes%d" % g, align_bytes=64))
+            g_scales.append(keep.tile([P, GROUP * IMAGES], U8, name="g_scales%d" % g, align_bytes=64))
+            k_grouped.append(keep.tile([P, GROUP, CHANNELS, PACK], BF16, name="k_grouped%d" % g, align_bytes=64))
         k_view = k_raw[:].rearrange("q t (c p) -> q p c t", p=FREQS)
         out_sb = keep.tile([P, CHANNELS, FREQS], F32, name="out_sb")
-        half = GROUP // 2
-        for g in range(GROUPS):
+        accs = []
+
+        def quantise_grad(g):
+            first = (g * GROUP) % BANK_FREQS
+            nc.vector.quantize_mx(
+                out=g_codes[g][:].bitcast(E5M2_X4),
+                scales=g_scales[g][:],
+                in_=g_grouped[g * GROUP // BANK_FREQS][:, first : first + GROUP, :].rearrange("q p m -> q (p m)"),
+            )
+
+        def regroup_k(g):
             first = g * GROUP
-            k_grouped = keep.tile([P, GROUP, CHANNELS, PACK], BF16, name="k_grouped%d" % g, align_bytes=64)
-            nc.vector.tensor_copy(out=k_grouped[:, :half], in_=k_view[:, first : first + half])
-            nc.scalar.copy(out=k_grouped[:, half:], in_=k_view[:, first + half : first + GROUP])
+            nc.vector.tensor_copy(out=k_grouped[g][:, :K_ON_VECTOR], in_=k_view[:, first : first + K_ON_VECTOR])
+            nc.scalar.copy(out=k_grouped[g][:, K_ON_VECTOR:], in_=k_view[:, first + K_ON_VECTOR : first + GROUP])
+
+        def quantise_k(g):
             for b in range(GROUP):
                 nc.vector.quantize_mx(
                     out=k_codes[g][:, b * PITCH : b * PITCH + CHANNELS].bitcast(E4M3_X4),
                     scales=k_scales[g][:, b * PITCH : b * PITCH + CHANNELS],
-                    in_=k_grouped[:, b].rearrange("q c t -> q (c t)"),
+                    in_=k_grouped[g][:, b].rearrange("q c t -> q (c t)"),
                 )
+
+        def multiply(g):
             acc = acc_pool.tile([P, N_MOVING], F32, name="acc")
             for b in range(GROUP):
                 window = slice(b * GAP, b * GAP + N_MOVING)
@@ -118,10 +128,17 @@ def tile_convdct_pa_s_kernel(tc, x_dct, k_dct, grad_out, out):
                     start=(b == 0),
                     stop=(b == GROUP - 1),
                 )
-            products = acc[:, : GROUP * CHANNELS].rearrange("n (b c) -> n c b", b=GROUP)
-            if g < GROUPS // 2:
-                nc.vector.tensor_copy(out=out_sb[:, :, first : first + GROUP], in_=products)
-            else:
-                nc.scalar.copy(out=out_sb[:, :, first : first + GROUP], in_=products)
+            accs.append(acc)
+
+        quantise_grad(0)
+        for g in range(GROUPS):
+            regroup_k(g)
+            if g + 1 < GROUPS:
+                quantise_grad(g + 1)
+            quantise_k(g)
+            multiply(g)
+        for g in range(GROUPS):
+            products = accs[g][:, : GROUP * CHANNELS].rearrange("n (b c) -> n c b", b=GROUP)
+            nc.scalar.copy(out=out_sb[:, :, g * GROUP : (g + 1) * GROUP], in_=products)
 
         nc.sync.dma_start(out=out.rearrange("n c h w -> n (c h w)"), in_=out_sb[:].rearrange("n c p -> n (c p)"))

@@ -30,6 +30,7 @@ N_MOVING = 512
 GAP = (GROUP - 1) * CHANNELS
 PITCH = CHANNELS + GAP
 STRIP = (GROUP - 1) * GAP + N_MOVING
+WARM_PASSES = 4
 K_ON_VECTOR = 1
 
 FLOPS = 2 * IMAGES * CHANNELS * FILTERS * FREQS
@@ -82,6 +83,18 @@ def tile_convdct_pa_s_kernel(tc, x_dct, k_dct, grad_out, out):
                     nc.vector.tensor_copy(out=dst, in_=src)
                 else:
                     nc.scalar.copy(out=dst, in_=src)
+
+        idle_bank = turned_pool.tile([P, N_MOVING], F32, name="turned")
+        for i in range(WARM_PASSES):
+            nc.tensor.matmul_mx(
+                out=idle_bank[:],
+                lhsT=k_codes[GROUPS - 1][:, :IMAGES].bitcast(E5M2_X4),
+                lhsT_scale=k_scales[GROUPS - 1][:, :IMAGES],
+                rhs=k_codes[GROUPS - 1][:, :N_MOVING].bitcast(E4M3_X4),
+                rhs_scale=k_scales[GROUPS - 1][:, :N_MOVING],
+                start=True,
+                stop=True,
+            )
 
         g_codes = []
         g_scales = []

@@ -30,8 +30,7 @@ N_MOVING = 512
 GAP = (GROUP - 1) * CHANNELS
 PITCH = CHANNELS + GAP
 STRIP = (GROUP - 1) * GAP + N_MOVING
-WARM_PASSES = 4
-K_ON_VECTOR = 1
+K_ON_VECTOR = 16
 
 FLOPS = 2 * IMAGES * CHANNELS * FILTERS * FREQS
 BYTES = 2 * IMAGES * FILTERS * FREQS + 2 * FILTERS * CHANNELS * FREQS + 4 * IMAGES * CHANNELS * FREQS
@@ -84,18 +83,6 @@ def tile_convdct_pa_s_kernel(tc, x_dct, k_dct, grad_out, out):
                 else:
                     nc.scalar.copy(out=dst, in_=src)
 
-        idle_bank = turned_pool.tile([P, N_MOVING], F32, name="turned")
-        for i in range(WARM_PASSES):
-            nc.tensor.matmul_mx(
-                out=idle_bank[:],
-                lhsT=k_codes[GROUPS - 1][:, :IMAGES].bitcast(E5M2_X4),
-                lhsT_scale=k_scales[GROUPS - 1][:, :IMAGES],
-                rhs=k_codes[GROUPS - 1][:, :N_MOVING].bitcast(E4M3_X4),
-                rhs_scale=k_scales[GROUPS - 1][:, :N_MOVING],
-                start=True,
-                stop=True,
-            )
-
         g_codes = []
         g_scales = []
         k_grouped = []
@@ -103,7 +90,7 @@ def tile_convdct_pa_s_kernel(tc, x_dct, k_dct, grad_out, out):
             g_codes.append(keep.tile([P, GROUP * IMAGES], U32, name="g_codes%d" % g, align_bytes=64))
             g_scales.append(keep.tile([P, GROUP * IMAGES], U8, name="g_scales%d" % g, align_bytes=64))
             k_grouped.append(keep.tile([P, GROUP, CHANNELS, PACK], BF16, name="k_grouped%d" % g, align_bytes=64))
-        k_view = k_raw[:].rearrange("q t (c p) -> q p c t", p=FREQS)
+        k_view = k_raw[:].rearrange("q t (c p) -> q c t p", p=FREQS)
         out_sb = keep.tile([P, CHANNELS, FREQS], F32, name="out_sb")
         accs = []
 
@@ -116,9 +103,10 @@ def tile_convdct_pa_s_kernel(tc, x_dct, k_dct, grad_out, out):
             )
 
         def regroup_k(g):
-            first = g * GROUP
-            nc.vector.tensor_copy(out=k_grouped[g][:, :K_ON_VECTOR], in_=k_view[:, first : first + K_ON_VECTOR])
-            nc.scalar.copy(out=k_grouped[g][:, K_ON_VECTOR:], in_=k_view[:, first + K_ON_VECTOR : first + GROUP])
+            src = k_view[:, :, :, g * GROUP : (g + 1) * GROUP]
+            dst = k_grouped[g][:].rearrange("q b c t -> q c t b")
+            nc.vector.tensor_copy(out=dst[:, :K_ON_VECTOR], in_=src[:, :K_ON_VECTOR])
+            nc.scalar.copy(out=dst[:, K_ON_VECTOR:], in_=src[:, K_ON_VECTOR:])
 
         def quantise_k(g):
             for b in range(GROUP):

@@ -30,7 +30,7 @@ N_MOVING = 512
 GAP = (GROUP - 1) * CHANNELS
 PITCH = CHANNELS + GAP
 STRIP = (GROUP - 1) * GAP + N_MOVING
-K_ON_VECTOR = 16
+K_ON_VECTOR = 24
 
 FLOPS = 2 * IMAGES * CHANNELS * FILTERS * FREQS
 BYTES = 2 * IMAGES * FILTERS * FREQS + 2 * FILTERS * CHANNELS * FREQS + 4 * IMAGES * CHANNELS * FREQS

@@ -30,6 +30,7 @@ N_MOVING = 512
 GAP = (GROUP - 1) * CHANNELS
 PITCH = CHANNELS + GAP
 STRIP = (GROUP - 1) * GAP + N_MOVING
+WARM_PASSES = 4
 K_ON_VECTOR = 24
 
 FLOPS = 2 * IMAGES * CHANNELS * FILTERS * FREQS
@@ -82,6 +83,18 @@ def tile_convdct_pa_s_kernel(tc, x_dct, k_dct, grad_out, out):
                     nc.vector.tensor_copy(out=dst, in_=src)
                 else:
                     nc.scalar.copy(out=dst, in_=src)
+
+        idle_bank = turned_pool.tile([P, N_MOVING], F32, name="turned")
+        for i in range(WARM_PASSES):
+            nc.tensor.matmul_mx(
+                out=idle_bank[:],
+                lhsT=k_codes[GROUPS - 1][:, :IMAGES].bitcast(E5M2_X4),
+                lhsT_scale=k_scales[GROUPS - 1][:, :IMAGES],
+                rhs=k_codes[GROUPS - 1][:, :N_MOVING].bitcast(E4M3_X4),
+                rhs_scale=k_scales[GROUPS - 1][:, :N_MOVING],
+                start=True,
+                stop=True,
+            )
 
         g_codes = []
         g_scales = []

@@ -27,9 +27,9 @@ BANKS = FREQS // BANK_FREQS
 GROUP = 4
 GROUPS = FREQS // GROUP
 N_MOVING = 512
-GAP = (GROUP - 1) * CHANNELS
-PITCH = CHANNELS + GAP
-STRIP = (GROUP - 1) * GAP + N_MOVING
+PAIR_SLOT = (1, 8)
+STRIP_SLOTS = 12
+STRIP = STRIP_SLOTS * CHANNELS
 WARM_PASSES = 4
 K_ON_VECTOR = 24
 
@@ -122,17 +122,19 @@ def tile_convdct_pa_s_kernel(tc, x_dct, k_dct, grad_out, out):
             nc.scalar.copy(out=dst[:, K_ON_VECTOR:], in_=src[:, K_ON_VECTOR:])
 
         def quantise_k(g):
-            for b in range(GROUP):
+            for u in range(GROUP // 2):
+                columns = slice(PAIR_SLOT[u] * CHANNELS, (PAIR_SLOT[u] + 2) * CHANNELS)
                 nc.vector.quantize_mx(
-                    out=k_codes[g][:, b * PITCH : b * PITCH + CHANNELS].bitcast(E4M3_X4),
-                    scales=k_scales[g][:, b * PITCH : b * PITCH + CHANNELS],
-                    in_=k_grouped[g][:, b].rearrange("q c t -> q (c t)"),
+                    out=k_codes[g][:, columns].bitcast(E4M3_X4),
+                    scales=k_scales[g][:, columns],
+                    in_=k_grouped[g][:, 2 * u : 2 * u + 2].rearrange("q b c t -> q (b c t)"),
                 )
 
         def multiply(g):
             acc = acc_pool.tile([P, N_MOVING], F32, name="acc")
             for b in range(GROUP):
-                window = slice(b * GAP, b * GAP + N_MOVING)
+                first_slot = PAIR_SLOT[b // 2] + b % 2 - 2 * b
+                window = slice(first_slot * CHANNELS, first_slot * CHANNELS + N_MOVING)
                 nc.tensor.matmul_mx(
                     out=acc[:],
                     lhsT=g_codes[g][:, b * IMAGES : (b + 1) * IMAGES].bitcast(E5M2_X4),
@@ -152,7 +154,7 @@ def tile_convdct_pa_s_kernel(tc, x_dct, k_dct, grad_out, out):
             quantise_k(g)
             multiply(g)
         for g in range(GROUPS):
-            products = accs[g][:, : GROUP * CHANNELS].rearrange("n (b c) -> n c b", b=GROUP)
+            products = accs[g][:].rearrange("n (b x c) -> n x c b", b=GROUP, x=2)[:, 0]
             nc.scalar.copy(out=out_sb[:, :, g * GROUP : (g + 1) * GROUP], in_=products)
 
         nc.sync.dma_start(out=out.rearrange("n c h w -> n (c h w)"), in_=out_sb[:].rearrange("n c p -> n (c p)"))

@@ -42,8 +42,8 @@ def tile_convdct_pa_s_kernel(tc, x_dct, k_dct, grad_out, out):
     with ExitStack() as ctx:
         ctx.enter_context(tc.manual_schedule())
         keep = ctx.enter_context(tc.tile_pool(name="keep", bufs=1))
-        turned_pool = ctx.enter_context(tc.psum_pool(name="turned_pool", bufs=4))
-        acc_pool = ctx.enter_context(tc.psum_pool(name="acc_pool", bufs=GROUPS))
+        turned_pool = ctx.enter_context(tc.psum_pool(name="banks", bufs=8))
+        acc_pool = turned_pool
 
         g_rows = grad_out.rearrange("n (t q) h w -> (n t) (q h w)", t=PACK)
         g_raw = []
@@ -131,7 +131,7 @@ def tile_convdct_pa_s_kernel(tc, x_dct, k_dct, grad_out, out):
                 )
 
         def multiply(g):
-            acc = acc_pool.tile([P, N_MOVING], F32, name="acc")
+            acc = acc_pool.tile([P, N_MOVING], F32, name="turned")
             for b in range(GROUP):
                 first_slot = PAIR_SLOT[b // 2] + b % 2 - 2 * b
                 window = slice(first_slot * CHANNELS, first_slot * CHANNELS + N_MOVING)

@@ -30,7 +30,7 @@ N_MOVING = 512
 PAIR_SLOT = (1, 8)
 STRIP_SLOTS = 12
 STRIP = STRIP_SLOTS * CHANNELS
-WARM_PASSES = 4
+WARM_PASSES = 6
 K_ON_VECTOR = 24
 
 FLOPS = 2 * IMAGES * CHANNELS * FILTERS * FREQS

@@ -27,11 +27,11 @@ BANKS = FREQS // BANK_FREQS
 GROUP = 4
 GROUPS = FREQS // GROUP
 N_MOVING = 512
-PAIR_SLOT = (1, 8)
-STRIP_SLOTS = 12
+PAIR_SLOT = (1, 9)
+STRIP_SLOTS = 13
 STRIP = STRIP_SLOTS * CHANNELS
 WARM_PASSES = 6
-K_ON_VECTOR = 24
+K_ON_VECTOR = 16
 
 FLOPS = 2 * IMAGES * CHANNELS * FILTERS * FREQS
 BYTES = 2 * IMAGES * FILTERS * FREQS + 2 * FILTERS * CHANNELS * FREQS + 4 * IMAGES * CHANNELS * FREQS
@@ -74,15 +74,20 @@ def tile_convdct_pa_s_kernel(tc, x_dct, k_dct, grad_out, out):
         for c in range(CHUNKS):
             words = g_raw[c][:].bitcast(F32).rearrange("r (q w) -> r w q", w=WORDS_PER_FILTER)
             for h in range(BANKS):
-                turned = turned_pool.tile([P, BANK_PAIRS * P], F32, name="turned")
-                for j in range(BANK_PAIRS):
-                    nc.tensor.transpose(turned[:, j * P : (j + 1) * P], words[:, h * BANK_PAIRS + j, :], ident[:])
-                src = turned[:].bitcast(BF16).rearrange("q (j m e) -> q j e m", j=BANK_PAIRS, e=2)
                 dst = g_grouped[h][:, :, c * P : (c + 1) * P].rearrange("q (j e) m -> q j e m", e=2)
-                if h % 2 == 0:
-                    nc.vector.tensor_copy(out=dst, in_=src)
-                else:
-                    nc.scalar.copy(out=dst, in_=src)
+                pieces = 2 if (h == 0 and c == CHUNKS - 1) else 1
+                pairs = BANK_PAIRS // pieces
+                for piece in range(pieces):
+                    turned = turned_pool.tile([P, BANK_PAIRS * P], F32, name="turned")
+                    for j in range(pairs):
+                        pair = h * BANK_PAIRS + piece * pairs + j
+                        nc.tensor.transpose(turned[:, j * P : (j + 1) * P], words[:, pair, :], ident[:])
+                    src = turned[:, : pairs * P].bitcast(BF16).rearrange("q (j m e) -> q j e m", j=pairs, e=2)
+                    some = dst[:, piece * pairs : (piece + 1) * pairs]
+                    if h % 2 == 0:
+                        nc.vector.tensor_copy(out=some, in_=src)
+                    else:
+                        nc.scalar.copy(out=some, in_=src)
 
         idle_bank = turned_pool.tile([P, N_MOVING], F32, name="turned")
         for i in range(WARM_PASSES):

from contextlib import ExitStack

import concourse.mybir as mybir
from concourse.masks import make_identity

BF16 = mybir.dt.bfloat16
F32 = mybir.dt.float32
I32 = mybir.dt.int32
U32 = mybir.dt.uint32
U8 = mybir.dt.uint8
E5M2_X4 = mybir.dt.float8_e5m2_x4
E4M3_X4 = mybir.dt.float8_e4m3fn_x4

IMAGES = 128
CHANNELS = 64
FILTERS = 512
FREQS = 16

P = 128
PACK = 4
CHUNK_IMAGES = P // PACK
CHUNKS = IMAGES // CHUNK_IMAGES
WORDS_PER_FILTER = FREQS // 2
BANK_PAIRS = 4
BANK_FREQS = 2 * BANK_PAIRS
BANKS = FREQS // BANK_FREQS
GROUP = 4
GROUPS = FREQS // GROUP
N_MOVING = 512
PAIR_SLOT = (1, 9)
STRIP_SLOTS = 13
STRIP = STRIP_SLOTS * CHANNELS
WARM_PASSES = 6
K_ON_VECTOR = 16

FLOPS = 2 * IMAGES * CHANNELS * FILTERS * FREQS
BYTES = 2 * IMAGES * FILTERS * FREQS + 2 * FILTERS * CHANNELS * FREQS + 4 * IMAGES * CHANNELS * FREQS


def tile_convdct_pa_s_kernel(tc, x_dct, k_dct, grad_out, out):
    nc = tc.nc
    with ExitStack() as ctx:
        ctx.enter_context(tc.manual_schedule())
        keep = ctx.enter_context(tc.tile_pool(name="keep", bufs=1))
        turned_pool = ctx.enter_context(tc.psum_pool(name="banks", bufs=8))
        acc_pool = turned_pool

        g_rows = grad_out.rearrange("n (t q) h w -> (n t) (q h w)", t=PACK)
        g_raw = []
        for c in range(CHUNKS):
            raw = keep.tile([P, P * FREQS], BF16, name="g_raw%d" % c)
            nc.sync.dma_start(out=raw[:], in_=g_rows[c * P : (c + 1) * P, :])
            g_raw.append(raw)
        k_raw = keep.tile([P, PACK, CHANNELS * FREQS], BF16, name="k_raw")
        nc.sync.dma_start(out=k_raw[:], in_=k_dct.rearrange("(t q) c h w -> q t (c h w)", q=P))

        ident = keep.tile([P, P], F32, name="ident")
        make_identity(nc, ident[:])

        k_codes = []
        k_scales = []
        for g in range(GROUPS):
            codes = keep.tile([P, STRIP], U32, name="k_codes%d" % g, align_bytes=64)
            scales = keep.tile([P, STRIP], U8, name="k_scales%d" % g, align_bytes=64)
            nc.vector.memset(codes[:].bitcast(I32), 0)
            nc.vector.memset(scales[:].bitcast(I32), 0)
            k_codes.append(codes)
            k_scales.append(scales)

        g_grouped = []
        for h in range(BANKS):
            grouped = keep.tile([P, BANK_FREQS, IMAGES * PACK], BF16, name="g_grouped%d" % h, align_bytes=64)
            g_grouped.append(grouped)
        for c in range(CHUNKS):
            words = g_raw[c][:].bitcast(F32).rearrange("r (q w) -> r w q", w=WORDS_PER_FILTER)
            for h in range(BANKS):
                dst = g_grouped[h][:, :, c * P : (c + 1) * P].rearrange("q (j e) m -> q j e m", e=2)
                pieces = 2 if (h == 0 and c == CHUNKS - 1) else 1
                pairs = BANK_PAIRS // pieces
                for piece in range(pieces):
                    turned = turned_pool.tile([P, BANK_PAIRS * P], F32, name="turned")
                    for j in range(pairs):
                        pair = h * BANK_PAIRS + piece * pairs + j
                        nc.tensor.transpose(turned[:, j * P : (j + 1) * P], words[:, pair, :], ident[:])
                    src = turned[:, : pairs * P].bitcast(BF16).rearrange("q (j m e) -> q j e m", j=pairs, e=2)
                    some = dst[:, piece * pairs : (piece + 1) * pairs]
                    if h % 2 == 0:
                        nc.vector.tensor_copy(out=some, in_=src)
                    else:
                        nc.scalar.copy(out=some, in_=src)

        idle_bank = turned_pool.tile([P, N_MOVING], F32, name="turned")
        for i in range(WARM_PASSES):
            nc.tensor.matmul_mx(
                out=idle_bank[:],
                lhsT=k_codes[GROUPS - 1][:, :IMAGES].bitcast(E5M2_X4),
                lhsT_scale=k_scales[GROUPS - 1][:, :IMAGES],
                rhs=k_codes[GROUPS - 1][:, :N_MOVING].bitcast(E4M3_X4),
                rhs_scale=k_scales[GROUPS - 1][:, :N_MOVING],
                start=True,
                stop=True,
            )

        g_codes = []
        g_scales = []
        k_grouped = []
        for g in range(GROUPS):
            g_codes.append(keep.tile([P, GROUP * IMAGES], U32, name="g_codes%d" % g, align_bytes=64))
            g_scales.append(keep.tile([P, GROUP * IMAGES], U8, name="g_scales%d" % g, align_bytes=64))
            k_grouped.append(keep.tile([P, GROUP, CHANNELS, PACK], BF16, name="k_grouped%d" % g, align_bytes=64))
        k_view = k_raw[:].rearrange("q t (c p) -> q c t p", p=FREQS)
        out_sb = keep.tile([P, CHANNELS, FREQS], F32, name="out_sb")
        accs = []

        def quantise_grad(g):
            first = (g * GROUP) % BANK_FREQS
            nc.vector.quantize_mx(
                out=g_codes[g][:].bitcast(E5M2_X4),
                scales=g_scales[g][:],
                in_=g_grouped[g * GROUP // BANK_FREQS][:, first : first + GROUP, :].rearrange("q p m -> q (p m)"),
            )

        def regroup_k(g):
            src = k_view[:, :, :, g * GROUP : (g + 1) * GROUP]
            dst = k_grouped[g][:].rearrange("q b c t -> q c t b")
            nc.vector.tensor_copy(out=dst[:, :K_ON_VECTOR], in_=src[:, :K_ON_VECTOR])
            nc.scalar.copy(out=dst[:, K_ON_VECTOR:], in_=src[:, K_ON_VECTOR:])

        def quantise_k(g):
            for u in range(GROUP // 2):
                columns = slice(PAIR_SLOT[u] * CHANNELS, (PAIR_SLOT[u] + 2) * CHANNELS)
                nc.vector.quantize_mx(
                    out=k_codes[g][:, columns].bitcast(E4M3_X4),
                    scales=k_scales[g][:, columns],
                    in_=k_grouped[g][:, 2 * u : 2 * u + 2].rearrange("q b c t -> q (b c t)"),
                )

        def multiply(g):
            acc = acc_pool.tile([P, N_MOVING], F32, name="turned")
            for b in range(GROUP):
                first_slot = PAIR_SLOT[b // 2] + b % 2 - 2 * b
                window = slice(first_slot * CHANNELS, first_slot * CHANNELS + N_MOVING)
                nc.tensor.matmul_mx(
                    out=acc[:],
                    lhsT=g_codes[g][:, b * IMAGES : (b + 1) * IMAGES].bitcast(E5M2_X4),
                    lhsT_scale=g_scales[g][:, b * IMAGES : (b + 1) * IMAGES],
                    rhs=k_codes[g][:, window].bitcast(E4M3_X4),
                    rhs_scale=k_scales[g][:, window],
                    start=(b == 0),
                    stop=(b == GROUP - 1),
                )
            accs.append(acc)

        quantise_grad(0)
        for g in range(GROUPS):
            regroup_k(g)
            if g + 1 < GROUPS:
                quantise_grad(g + 1)
            quantise_k(g)
            multiply(g)
        for g in range(GROUPS):
            products = accs[g][:].rearrange("n (b x c) -> n x c b", b=GROUP, x=2)[:, 0]
            nc.scalar.copy(out=out_sb[:, :, g * GROUP : (g + 1) * GROUP], in_=products)

        nc.sync.dma_start(out=out.rearrange("n c h w -> n (c h w)"), in_=out_sb[:].rearrange("n c p -> n (c p)"))
